import numpy as np
import ml_dtypes


def mxq(x, axis, fmt="e4m3"):
    dtype, down = {"e4m3": (ml_dtypes.float8_e4m3fn, 7), "e5m2": (ml_dtypes.float8_e5m2, 14)}[fmt]
    v = np.moveaxis(np.asarray(x, np.float32).astype(ml_dtypes.bfloat16).astype(np.float64), axis, -1)
    blocks = v.reshape(v.shape[:-1] + (-1, 32))
    amax = np.abs(blocks).max(-1, keepdims=True)
    byte = np.maximum(np.where(amax > 0, np.frexp(amax)[1] - 1 + 127, 0) - down, 1)
    scale = np.exp2(byte - 127.0)
    codes = (blocks / scale).astype(np.float32).astype(dtype).astype(np.float64)
    return np.moveaxis((codes * scale).reshape(v.shape), -1, axis)


WIDE = False


def mx_kscale(k):
    if not WIDE:
        return np.ones(k)
    levels = np.array([10, -10, 5, -5, 0])
    a = np.random.permutation(np.resize(levels, k // 512 * 4)).reshape(k // 512, 4)
    idx = np.arange(k)
    return np.exp2(a[idx // 512, idx % 128 // 32])


BF16 = ml_dtypes.bfloat16


def bf(x):
    return np.asarray(x, np.float32).astype(BF16)


def f64(x):
    return np.asarray(x).astype(np.float64)


B, N, NIN, CTX, H, NOUT = 2, 64, 512, 3, 512, 2
F = NIN * CTX


def shift_down(y, d):
    return np.pad(y[:, :-d, :], ((0, 0), (d, 0), (0, 0)))


def shift_up(y, d):
    return np.pad(y[:, d:, :], ((0, 0), (0, d), (0, 0)))


def context_linear(xq, w, shifts):
    y = xq @ mxq(w[:, :NIN].T, 0, "e4m3")
    c = 1
    for d in range(1, CTX // 2 + 1):
        for shift in shifts:
            y = y + shift(xq @ mxq(w[:, c * NIN:(c + 1) * NIN].T, 0, "e4m3"), d)
            c += 1
    return y


def setup_inputs():
    s, u = mx_kscale(NIN), mx_kscale(H)
    return {"x_l": bf(np.random.standard_normal((B, N, NIN)) * s),
            "W_l": bf(np.random.standard_normal((H, F)) / np.sqrt(F) / np.tile(s, CTX) * u[:, None]),
            "b_l": bf(np.random.standard_normal(H) * 0.3 * u),
            "W_bil": bf(np.random.standard_normal((NOUT, H, H)) * 0.2 / np.sqrt(H) / u[None, :, None])}


def reference(x_l, W_l, b_l, W_bil):
    xq = mxq(f64(x_l), 2, "e4m3")
    hl = np.maximum(context_linear(xq, f64(W_l), (shift_down, shift_up)) + f64(b_l), 0.0)
    wb = f64(W_bil).transpose(1, 0, 2).reshape(H, NOUT * H)
    t = mxq(hl, 2, "e4m3") @ mxq(wb, 0, "e4m3")
    return t.reshape(B, N, NOUT, H)

@@ -1,0 +1,176 @@
+from contextlib import ExitStack
+
+import concourse.mybir as mybir
+from concourse.masks import make_identity
+
+F32 = mybir.dt.float32
+BF16 = mybir.dt.bfloat16
+U32 = mybir.dt.uint32
+U8 = mybir.dt.uint8
+FP8X4 = mybir.dt.float8_e4m3fn_x4
+RELU = mybir.ActivationFunctionType.Relu
+
+P = 128
+PACK = 4
+BATCH = 2
+SEQ = 64
+TOK = BATCH * SEQ
+NIN = 512
+WINDOWS = 3
+H = 512
+H_TILES = H // P
+NOUT = 2
+
+HALVES = 2
+ITEMS = H_TILES * WINDOWS
+ITEMS_PER_BANK = 2
+WL_BANKS = ITEMS // ITEMS_PER_BANK
+WL_CHUNK = ITEMS_PER_BANK * NIN
+BANKS_PER_ROUND = 3
+TILES_PER_ROUND = 2
+
+UNIT = 256
+UNITS = NOUT * H // UNIT
+UNITS_PER_MAP = H // UNIT
+VECTOR_COLS = 160
+
+FLOPS = 2 * TOK * (WINDOWS * NIN) * H + 2 * TOK * H * (NOUT * H)
+
+
+def tile_bilinearpairedlayer_pa_s_kernel(tc, x_l, W_l, b_l, W_bil, out):
+    nc = tc.nc
+    with ExitStack() as ctx:
+        keep = ctx.enter_context(tc.tile_pool(name="keep", bufs=1))
+        psum_x = ctx.enter_context(tc.psum_pool(name="psum_x", bufs=1))
+        psum_w = ctx.enter_context(tc.psum_pool(name="psum_w", bufs=3))
+        psum_pre = ctx.enter_context(tc.psum_pool(name="psum_pre", bufs=2))
+        psum_out = ctx.enter_context(tc.psum_pool(name="psum_out", bufs=2))
+
+        x_raw = keep.tile([P, NIN], BF16)
+        nc.sync.dma_start(out=x_raw[:], in_=x_l.rearrange("b i f -> (b i) f"))
+        bias = keep.tile([P, PACK], BF16)
+        nc.scalar.dma_start(out=bias[:], in_=b_l.rearrange("(p t) -> p t", t=PACK))
+        wl_rows = W_l.rearrange("(p t) f -> p (t f)", t=PACK)
+        wl_raw = []
+        for n in range(WL_BANKS):
+            chunk = keep.tile([P, WL_CHUNK], BF16, name="wl_raw%d" % n)
+            nc.sync.dma_start(out=chunk[:], in_=wl_rows[:, n * WL_CHUNK : (n + 1) * WL_CHUNK])
+            wl_raw.append(chunk)
+        wb_raw = []
+        for k in range(NOUT):
+            chunk = keep.tile([P, PACK, H], BF16, name="wb_raw%d" % k)
+            nc.sync.dma_start(out=chunk[:], in_=W_bil[k].rearrange("(p t) g -> p t g", t=PACK))
+            wb_raw.append(chunk)
+
+        ident = keep.tile([P, P], F32)
+        make_identity(nc, ident[:])
+
+        x_grouped = keep.tile([P, WINDOWS * TOK * PACK], BF16, align_bytes=64)
+        nc.vector.memset(x_grouped[:], 0.0)
+        x_words = x_raw[:].bitcast(F32)
+        xT = psum_x.tile([P, HALVES, TOK], F32)
+        for u in range(HALVES):
+            nc.tensor.transpose(xT[:, u, :], x_words[:, u * P : (u + 1) * P], ident[:])
+        xT_view = xT[:].rearrange("p u (b i) -> p b i u", b=BATCH)
+        xg_words = x_grouped[:].bitcast(F32).rearrange(
+            "p (c b i u) -> p c b i u", c=WINDOWS, b=BATCH, u=HALVES
+        )
+        nc.vector.tensor_copy(out=xg_words[:, 0], in_=xT_view)
+        nc.vector.tensor_copy(out=xg_words[:, 1, :, 1:SEQ, :], in_=xT_view[:, :, 0 : SEQ - 1, :])
+        nc.vector.tensor_copy(out=xg_words[:, 2, :, 0 : SEQ - 1, :], in_=xT_view[:, :, 1:SEQ, :])
+        x_codes = keep.tile([P, WINDOWS, TOK], U32, align_bytes=64)
+        x_scales = keep.tile([P, WINDOWS, TOK], U8, align_bytes=64)
+        for c in range(WINDOWS):
+            nc.vector.quantize_mx(
+                out=x_codes[:, c, :].bitcast(FP8X4),
+                scales=x_scales[:, c, :],
+                in_=x_grouped[:, c * TOK * PACK : (c + 1) * TOK * PACK],
+            )
+
+        wl_grouped = keep.tile([P, ITEMS * P * PACK], BF16, align_bytes=64)
+        wlg_words = wl_grouped[:].bitcast(F32).rearrange("p (a h u) -> p a h u", a=ITEMS, u=HALVES)
+        wl_codes = keep.tile([P, ITEMS * P], U32, align_bytes=64)
+        wl_scales = keep.tile([P, ITEMS * P], U8, align_bytes=64)
+        hlT = keep.tile([P, H_TILES, TOK], BF16)
+        for r in range(H_TILES // TILES_PER_ROUND):
+            for n in range(r * BANKS_PER_ROUND, (r + 1) * BANKS_PER_ROUND):
+                wl_words = wl_raw[n][:].bitcast(F32)
+                wT = psum_w.tile([P, ITEMS_PER_BANK * HALVES, P], F32)
+                for j in range(ITEMS_PER_BANK * HALVES):
+                    nc.tensor.transpose(wT[:, j, :], wl_words[:, j * P : (j + 1) * P], ident[:])
+                items = slice(n * ITEMS_PER_BANK, (n + 1) * ITEMS_PER_BANK)
+                nc.scalar.copy(
+                    out=wlg_words[:, items, :, :],
+                    in_=wT[:].rearrange("p (a u) h -> p a h u", u=HALVES),
+                )
+                nc.vector.quantize_mx(
+                    out=wl_codes[:, n * ITEMS_PER_BANK * P : (n + 1) * ITEMS_PER_BANK * P].bitcast(FP8X4),
+                    scales=wl_scales[:, n * ITEMS_PER_BANK * P : (n + 1) * ITEMS_PER_BANK * P],
+                    in_=wl_grouped[:, n * WL_CHUNK : (n + 1) * WL_CHUNK],
+                )
+            pre = psum_pre.tile([P, TILES_PER_ROUND, TOK], F32)
+            for j in range(TILES_PER_ROUND):
+                t = r * TILES_PER_ROUND + j
+                for c in range(WINDOWS):
+                    a = t * WINDOWS + c
+                    nc.tensor.matmul_mx(
+                        out=pre[:, j, :],
+                        lhsT=wl_codes[:, a * P : (a + 1) * P].bitcast(FP8X4),
+                        lhsT_scale=wl_scales[:, a * P : (a + 1) * P],
+                        rhs=x_codes[:, c, :].bitcast(FP8X4),
+                        rhs_scale=x_scales[:, c, :],
+                        start=(c == 0),
+                        stop=(c == WINDOWS - 1),
+                    )
+            for j in range(TILES_PER_ROUND):
+                t = r * TILES_PER_ROUND + j
+                nc.scalar.activation(
+                    out=hlT[:, t, :], in_=pre[:, j, :], func=RELU, bias=bias[:, t : t + 1], scale=1.0
+                )
+
+        hl_grouped = keep.tile([P, TOK, PACK], BF16, align_bytes=64)
+        nc.vector.tensor_copy(out=hl_grouped[:], in_=hlT[:].rearrange("p t r -> p r t"))
+        hl_codes = keep.tile([P, TOK], U32, align_bytes=64)
+        hl_scales = keep.tile([P, TOK], U8, align_bytes=64)
+        nc.vector.quantize_mx(
+            out=hl_codes[:].bitcast(FP8X4),
+            scales=hl_scales[:],
+            in_=hl_grouped[:].rearrange("p r t -> p (r t)"),
+        )
+
+        out_rows = out.rearrange("b i k g -> (b i) (k g)")
+        wb_codes = keep.tile([P, UNITS, UNIT], U32, align_bytes=64)
+        wb_scales = keep.tile([P, UNITS, UNIT], U8, align_bytes=64)
+        for q in range(UNITS):
+            k = q // UNITS_PER_MAP
+            g0 = (q % UNITS_PER_MAP) * UNIT
+            wb_grouped = keep.tile([P, UNIT, PACK], BF16, align_bytes=64, name="wb_grouped%d" % q)
+            nc.vector.tensor_copy(
+                out=wb_grouped[:, 0:VECTOR_COLS, :].rearrange("p (c i) t -> p c t i", i=4),
+                in_=wb_raw[k][:, :, g0 : g0 + VECTOR_COLS].rearrange("p t (c i) -> p c t i", i=4),
+            )
+            nc.scalar.copy(
+                out=wb_grouped[:, VECTOR_COLS:UNIT, :].rearrange("p (c i) t -> p c t i", i=4),
+                in_=wb_raw[k][:, :, g0 + VECTOR_COLS : g0 + UNIT].rearrange("p t (c i) -> p c t i", i=4),
+            )
+            nc.vector.quantize_mx(
+                out=wb_codes[:, q, :].bitcast(FP8X4),
+                scales=wb_scales[:, q, :],
+                in_=wb_grouped[:].rearrange("p g t -> p (g t)"),
+            )
+            acc = psum_out.tile([P, UNIT], F32)
+            nc.tensor.matmul_mx(
+                out=acc[:],
+                lhsT=hl_codes[:].bitcast(FP8X4),
+                lhsT_scale=hl_scales[:],
+                rhs=wb_codes[:, q, :].bitcast(FP8X4),
+                rhs_scale=wb_scales[:, q, :],
+                start=True,
+                stop=True,
+            )
+            result = keep.tile([P, UNIT], F32, name="result%d" % q)
+            if q % 2 == 0:
+                nc.scalar.copy(out=result[:], in_=acc[:])
+            else:
+                nc.vector.tensor_copy(out=result[:], in_=acc[:])
+            nc.sync.dma_start(out=out_rows[:, q * UNIT : (q + 1) * UNIT], in_=result[:])

@@ -26,8 +26,6 @@ ITEMS = H_TILES * WINDOWS
 ITEMS_PER_BANK = 2
 WL_BANKS = ITEMS // ITEMS_PER_BANK
 WL_CHUNK = ITEMS_PER_BANK * NIN
-BANKS_PER_ROUND = 3
-TILES_PER_ROUND = 2
 
 UNIT = 256
 UNITS = NOUT * H // UNIT
@@ -45,6 +43,7 @@ def tile_bilinearpairedlayer_pa_s_kernel(tc, x_l, W_l, b_l, W_bil, out):
         psum_w = ctx.enter_context(tc.psum_pool(name="psum_w", bufs=3))
         psum_pre = ctx.enter_context(tc.psum_pool(name="psum_pre", bufs=2))
         psum_out = ctx.enter_context(tc.psum_pool(name="psum_out", bufs=2))
+        ctx.enter_context(tc.manual_schedule())
 
         x_raw = keep.tile([P, NIN], BF16)
         nc.sync.dma_start(out=x_raw[:], in_=x_l.rearrange("b i f -> (b i) f"))
@@ -91,73 +90,78 @@ def tile_bilinearpairedlayer_pa_s_kernel(tc, x_l, W_l, b_l, W_bil, out):
         wlg_words = wl_grouped[:].bitcast(F32).rearrange("p (a h u) -> p a h u", a=ITEMS, u=HALVES)
         wl_codes = keep.tile([P, ITEMS * P], U32, align_bytes=64)
         wl_scales = keep.tile([P, ITEMS * P], U8, align_bytes=64)
+        for n in range(WL_BANKS):
+            wl_words = wl_raw[n][:].bitcast(F32)
+            wT = psum_w.tile([P, ITEMS_PER_BANK * HALVES, P], F32)
+            for j in range(ITEMS_PER_BANK * HALVES):
+                nc.tensor.transpose(wT[:, j, :], wl_words[:, j * P : (j + 1) * P], ident[:])
+            nc.scalar.copy(
+                out=wlg_words[:, n * ITEMS_PER_BANK : (n + 1) * ITEMS_PER_BANK, :, :],
+                in_=wT[:].rearrange("p (a u) h -> p a h u", u=HALVES),
+            )
+            nc.vector.quantize_mx(
+                out=wl_codes[:, n * ITEMS_PER_BANK * P : (n + 1) * ITEMS_PER_BANK * P].bitcast(FP8X4),
+                scales=wl_scales[:, n * ITEMS_PER_BANK * P : (n + 1) * ITEMS_PER_BANK * P],
+                in_=wl_grouped[:, n * WL_CHUNK : (n + 1) * WL_CHUNK],
+            )
+
         hlT = keep.tile([P, H_TILES, TOK], BF16)
-        for r in range(H_TILES // TILES_PER_ROUND):
-            for n in range(r * BANKS_PER_ROUND, (r + 1) * BANKS_PER_ROUND):
-                wl_words = wl_raw[n][:].bitcast(F32)
-                wT = psum_w.tile([P, ITEMS_PER_BANK * HALVES, P], F32)
-                for j in range(ITEMS_PER_BANK * HALVES):
-                    nc.tensor.transpose(wT[:, j, :], wl_words[:, j * P : (j + 1) * P], ident[:])
-                items = slice(n * ITEMS_PER_BANK, (n + 1) * ITEMS_PER_BANK)
-                nc.scalar.copy(
-                    out=wlg_words[:, items, :, :],
-                    in_=wT[:].rearrange("p (a u) h -> p a h u", u=HALVES),
-                )
-                nc.vector.quantize_mx(
-                    out=wl_codes[:, n * ITEMS_PER_BANK * P : (n + 1) * ITEMS_PER_BANK * P].bitcast(FP8X4),
-                    scales=wl_scales[:, n * ITEMS_PER_BANK * P : (n + 1) * ITEMS_PER_BANK * P],
-                    in_=wl_grouped[:, n * WL_CHUNK : (n + 1) * WL_CHUNK],
-                )
-            pre = psum_pre.tile([P, TILES_PER_ROUND, TOK], F32)
-            for j in range(TILES_PER_ROUND):
-                t = r * TILES_PER_ROUND + j
-                for c in range(WINDOWS):
-                    a = t * WINDOWS + c
-                    nc.tensor.matmul_mx(
-                        out=pre[:, j, :],
-                        lhsT=wl_codes[:, a * P : (a + 1) * P].bitcast(FP8X4),
-                        lhsT_scale=wl_scales[:, a * P : (a + 1) * P],
-                        rhs=x_codes[:, c, :].bitcast(FP8X4),
-                        rhs_scale=x_scales[:, c, :],
-                        start=(c == 0),
-                        stop=(c == WINDOWS - 1),
-                    )
-            for j in range(TILES_PER_ROUND):
-                t = r * TILES_PER_ROUND + j
-                nc.scalar.activation(
-                    out=hlT[:, t, :], in_=pre[:, j, :], func=RELU, bias=bias[:, t : t + 1], scale=1.0
-                )
 
-        hl_grouped = keep.tile([P, TOK, PACK], BF16, align_bytes=64)
-        nc.vector.tensor_copy(out=hl_grouped[:], in_=hlT[:].rearrange("p t r -> p r t"))
-        hl_codes = keep.tile([P, TOK], U32, align_bytes=64)
-        hl_scales = keep.tile([P, TOK], U8, align_bytes=64)
-        nc.vector.quantize_mx(
-            out=hl_codes[:].bitcast(FP8X4),
-            scales=hl_scales[:],
-            in_=hl_grouped[:].rearrange("p r t -> p (r t)"),
-        )
+        def layer1_tile(t):
+            pre = psum_pre.tile([P, TOK], F32)
+            for c in range(WINDOWS):
+                a = t * WINDOWS + c
+                nc.tensor.matmul_mx(
+                    out=pre[:],
+                    lhsT=wl_codes[:, a * P : (a + 1) * P].bitcast(FP8X4),
+                    lhsT_scale=wl_scales[:, a * P : (a + 1) * P],
+                    rhs=x_codes[:, c, :].bitcast(FP8X4),
+                    rhs_scale=x_scales[:, c, :],
+                    start=(c == 0),
+                    stop=(c == WINDOWS - 1),
+                )
+            nc.scalar.activation(
+                out=hlT[:, t, :], in_=pre[:], func=RELU, bias=bias[:, t : t + 1], scale=1.0
+            )
 
-        out_rows = out.rearrange("b i k g -> (b i) (k g)")
+        wb_grouped = keep.tile([P, UNITS, UNIT, PACK], BF16, align_bytes=64)
         wb_codes = keep.tile([P, UNITS, UNIT], U32, align_bytes=64)
         wb_scales = keep.tile([P, UNITS, UNIT], U8, align_bytes=64)
-        for q in range(UNITS):
-            k = q // UNITS_PER_MAP
+
+        def regroup_unit(q):
+            raw = wb_raw[q // UNITS_PER_MAP]
             g0 = (q % UNITS_PER_MAP) * UNIT
-            wb_grouped = keep.tile([P, UNIT, PACK], BF16, align_bytes=64, name="wb_grouped%d" % q)
             nc.vector.tensor_copy(
-                out=wb_grouped[:, 0:VECTOR_COLS, :].rearrange("p (c i) t -> p c t i", i=4),
-                in_=wb_raw[k][:, :, g0 : g0 + VECTOR_COLS].rearrange("p t (c i) -> p c t i", i=4),
+                out=wb_grouped[:, q, 0:VECTOR_COLS, :].rearrange("p (c i) t -> p c t i", i=4),
+                in_=raw[:, :, g0 : g0 + VECTOR_COLS].rearrange("p t (c i) -> p c t i", i=4),
             )
             nc.scalar.copy(
-                out=wb_grouped[:, VECTOR_COLS:UNIT, :].rearrange("p (c i) t -> p c t i", i=4),
-                in_=wb_raw[k][:, :, g0 + VECTOR_COLS : g0 + UNIT].rearrange("p t (c i) -> p c t i", i=4),
+                out=wb_grouped[:, q, VECTOR_COLS:UNIT, :].rearrange("p (c i) t -> p c t i", i=4),
+                in_=raw[:, :, g0 + VECTOR_COLS : g0 + UNIT].rearrange("p t (c i) -> p c t i", i=4),
             )
+
+        def quantise_unit(q):
             nc.vector.quantize_mx(
                 out=wb_codes[:, q, :].bitcast(FP8X4),
                 scales=wb_scales[:, q, :],
-                in_=wb_grouped[:].rearrange("p g t -> p (g t)"),
+                in_=wb_grouped[:, q, :, :].rearrange("p g t -> p (g t)"),
             )
+
+        hl_grouped = keep.tile([P, TOK, PACK], BF16, align_bytes=64)
+        hl_codes = keep.tile([P, TOK], U32, align_bytes=64)
+        hl_scales = keep.tile([P, TOK], U8, align_bytes=64)
+
+        def quantise_hl():
+            nc.vector.tensor_copy(out=hl_grouped[:], in_=hlT[:].rearrange("p t r -> p r t"))
+            nc.vector.quantize_mx(
+                out=hl_codes[:].bitcast(FP8X4),
+                scales=hl_scales[:],
+                in_=hl_grouped[:].rearrange("p r t -> p (r t)"),
+            )
+
+        out_rows = out.rearrange("b i k g -> (b i) (k g)")
+
+        def layer2_unit(q):
             acc = psum_out.tile([P, UNIT], F32)
             nc.tensor.matmul_mx(
                 out=acc[:],
@@ -174,3 +178,18 @@ def tile_bilinearpairedlayer_pa_s_kernel(tc, x_l, W_l, b_l, W_bil, out):
             else:
                 nc.vector.tensor_copy(out=result[:], in_=acc[:])
             nc.sync.dma_start(out=out_rows[:, q * UNIT : (q + 1) * UNIT], in_=result[:])
+
+        for t in range(H_TILES - 1):
+            layer1_tile(t)
+        regroup_unit(0)
+        layer1_tile(H_TILES - 1)
+        regroup_unit(1)
+        quantise_unit(0)
+        quantise_hl()
+        quantise_unit(1)
+        regroup_unit(2)
+        regroup_unit(3)
+        quantise_unit(2)
+        quantise_unit(3)
+        for q in range(UNITS):
+            layer2_unit(q)

@@ -64,6 +64,11 @@ def tile_bilinearpairedlayer_pa_s_kernel(tc, x_l, W_l, b_l, W_bil, out):
         ident = keep.tile([P, P], F32)
         make_identity(nc, ident[:])
 
+        warm_in = keep.tile([P, 1], F32)
+        warm_out = keep.tile([P, 1], F32)
+        nc.vector.memset(warm_in[:], 0.0)
+        nc.scalar.activation(out=warm_out[:], in_=warm_in[:], func=RELU)
+
         x_grouped = keep.tile([P, WINDOWS * TOK * PACK], BF16, align_bytes=64)
         nc.vector.memset(x_grouped[:], 0.0)
         x_words = x_raw[:].bitcast(F32)

@@ -39,10 +39,8 @@ def tile_bilinearpairedlayer_pa_s_kernel(tc, x_l, W_l, b_l, W_bil, out):
     nc = tc.nc
     with ExitStack() as ctx:
         keep = ctx.enter_context(tc.tile_pool(name="keep", bufs=1))
-        psum_x = ctx.enter_context(tc.psum_pool(name="psum_x", bufs=1))
-        psum_w = ctx.enter_context(tc.psum_pool(name="psum_w", bufs=3))
-        psum_pre = ctx.enter_context(tc.psum_pool(name="psum_pre", bufs=2))
-        psum_out = ctx.enter_context(tc.psum_pool(name="psum_out", bufs=2))
+        psum_one = ctx.enter_context(tc.psum_pool(name="psum_one", bufs=6))
+        psum_two = ctx.enter_context(tc.psum_pool(name="psum_two", bufs=2))
         ctx.enter_context(tc.manual_schedule())
 
         x_raw = keep.tile([P, NIN], BF16)
@@ -64,15 +62,10 @@ def tile_bilinearpairedlayer_pa_s_kernel(tc, x_l, W_l, b_l, W_bil, out):
         ident = keep.tile([P, P], F32)
         make_identity(nc, ident[:])
 
-        warm_in = keep.tile([P, 1], F32)
-        warm_out = keep.tile([P, 1], F32)
-        nc.vector.memset(warm_in[:], 0.0)
-        nc.scalar.activation(out=warm_out[:], in_=warm_in[:], func=RELU)
-
         x_grouped = keep.tile([P, WINDOWS * TOK * PACK], BF16, align_bytes=64)
         nc.vector.memset(x_grouped[:], 0.0)
         x_words = x_raw[:].bitcast(F32)
-        xT = psum_x.tile([P, HALVES, TOK], F32)
+        xT = psum_one.tile([P, HALVES, TOK], F32, tag="bank")
         for u in range(HALVES):
             nc.tensor.transpose(xT[:, u, :], x_words[:, u * P : (u + 1) * P], ident[:])
         xT_view = xT[:].rearrange("p u (b i) -> p b i u", b=BATCH)
@@ -97,7 +90,7 @@ def tile_bilinearpairedlayer_pa_s_kernel(tc, x_l, W_l, b_l, W_bil, out):
         wl_scales = keep.tile([P, ITEMS * P], U8, align_bytes=64)
         for n in range(WL_BANKS):
             wl_words = wl_raw[n][:].bitcast(F32)
-            wT = psum_w.tile([P, ITEMS_PER_BANK * HALVES, P], F32)
+            wT = psum_one.tile([P, ITEMS_PER_BANK * HALVES, P], F32, tag="bank")
             for j in range(ITEMS_PER_BANK * HALVES):
                 nc.tensor.transpose(wT[:, j, :], wl_words[:, j * P : (j + 1) * P], ident[:])
             nc.scalar.copy(
@@ -113,7 +106,7 @@ def tile_bilinearpairedlayer_pa_s_kernel(tc, x_l, W_l, b_l, W_bil, out):
         hlT = keep.tile([P, H_TILES, TOK], BF16)
 
         def layer1_tile(t):
-            pre = psum_pre.tile([P, TOK], F32)
+            pre = psum_one.tile([P, TOK], F32, tag="bank")
             for c in range(WINDOWS):
                 a = t * WINDOWS + c
                 nc.tensor.matmul_mx(
@@ -125,6 +118,9 @@ def tile_bilinearpairedlayer_pa_s_kernel(tc, x_l, W_l, b_l, W_bil, out):
                     start=(c == 0),
                     stop=(c == WINDOWS - 1),
                 )
+            return pre
+
+        def relu_tile(t, pre):
             nc.scalar.activation(
                 out=hlT[:, t, :], in_=pre[:], func=RELU, bias=bias[:, t : t + 1], scale=1.0
             )
@@ -156,8 +152,10 @@ def tile_bilinearpairedlayer_pa_s_kernel(tc, x_l, W_l, b_l, W_bil, out):
         hl_codes = keep.tile([P, TOK], U32, align_bytes=64)
         hl_scales = keep.tile([P, TOK], U8, align_bytes=64)
 
-        def quantise_hl():
+        def regroup_hl():
             nc.vector.tensor_copy(out=hl_grouped[:], in_=hlT[:].rearrange("p t r -> p r t"))
+
+        def quantise_hl():
             nc.vector.quantize_mx(
                 out=hl_codes[:].bitcast(FP8X4),
                 scales=hl_scales[:],
@@ -167,7 +165,7 @@ def tile_bilinearpairedlayer_pa_s_kernel(tc, x_l, W_l, b_l, W_bil, out):
         out_rows = out.rearrange("b i k g -> (b i) (k g)")
 
         def layer2_unit(q):
-            acc = psum_out.tile([P, UNIT], F32)
+            acc = psum_two.tile([P, UNIT], F32)
             nc.tensor.matmul_mx(
                 out=acc[:],
                 lhsT=hl_codes[:].bitcast(FP8X4),
@@ -184,15 +182,15 @@ def tile_bilinearpairedlayer_pa_s_kernel(tc, x_l, W_l, b_l, W_bil, out):
                 nc.vector.tensor_copy(out=result[:], in_=acc[:])
             nc.sync.dma_start(out=out_rows[:, q * UNIT : (q + 1) * UNIT], in_=result[:])
 
-        for t in range(H_TILES - 1):
-            layer1_tile(t)
         regroup_unit(0)
-        layer1_tile(H_TILES - 1)
+        for t in range(H_TILES):
+            relu_tile(t, layer1_tile(t))
         regroup_unit(1)
-        quantise_unit(0)
-        quantise_hl()
-        quantise_unit(1)
         regroup_unit(2)
+        quantise_unit(0)
+        regroup_hl()
+        quantise_unit(1)
+        quantise_hl()
         regroup_unit(3)
         quantise_unit(2)
         quantise_unit(3)

from contextlib import ExitStack

import concourse.mybir as mybir
from concourse.masks import make_identity

F32 = mybir.dt.float32
BF16 = mybir.dt.bfloat16
U32 = mybir.dt.uint32
U8 = mybir.dt.uint8
FP8X4 = mybir.dt.float8_e4m3fn_x4
RELU = mybir.ActivationFunctionType.Relu

P = 128
PACK = 4
BATCH = 2
SEQ = 64
TOK = BATCH * SEQ
NIN = 512
WINDOWS = 3
H = 512
H_TILES = H // P
NOUT = 2

HALVES = 2
ITEMS = H_TILES * WINDOWS
ITEMS_PER_BANK = 2
WL_BANKS = ITEMS // ITEMS_PER_BANK
WL_CHUNK = ITEMS_PER_BANK * NIN

UNIT = 256
UNITS = NOUT * H // UNIT
UNITS_PER_MAP = H // UNIT
VECTOR_COLS = 160

FLOPS = 2 * TOK * (WINDOWS * NIN) * H + 2 * TOK * H * (NOUT * H)


def tile_bilinearpairedlayer_pa_s_kernel(tc, x_l, W_l, b_l, W_bil, out):
    nc = tc.nc
    with ExitStack() as ctx:
        keep = ctx.enter_context(tc.tile_pool(name="keep", bufs=1))
        psum_one = ctx.enter_context(tc.psum_pool(name="psum_one", bufs=6))
        psum_two = ctx.enter_context(tc.psum_pool(name="psum_two", bufs=2))
        ctx.enter_context(tc.manual_schedule())

        x_raw = keep.tile([P, NIN], BF16)
        nc.sync.dma_start(out=x_raw[:], in_=x_l.rearrange("b i f -> (b i) f"))
        bias = keep.tile([P, PACK], BF16)
        nc.scalar.dma_start(out=bias[:], in_=b_l.rearrange("(p t) -> p t", t=PACK))
        wl_rows = W_l.rearrange("(p t) f -> p (t f)", t=PACK)
        wl_raw = []
        for n in range(WL_BANKS):
            chunk = keep.tile([P, WL_CHUNK], BF16, name="wl_raw%d" % n)
            nc.sync.dma_start(out=chunk[:], in_=wl_rows[:, n * WL_CHUNK : (n + 1) * WL_CHUNK])
            wl_raw.append(chunk)
        wb_raw = []
        for k in range(NOUT):
            chunk = keep.tile([P, PACK, H], BF16, name="wb_raw%d" % k)
            nc.sync.dma_start(out=chunk[:], in_=W_bil[k].rearrange("(p t) g -> p t g", t=PACK))
            wb_raw.append(chunk)

        ident = keep.tile([P, P], F32)
        make_identity(nc, ident[:])

        x_grouped = keep.tile([P, WINDOWS * TOK * PACK], BF16, align_bytes=64)
        nc.vector.memset(x_grouped[:], 0.0)
        x_words = x_raw[:].bitcast(F32)
        xT = psum_one.tile([P, HALVES, TOK], F32, tag="bank")
        for u in range(HALVES):
            nc.tensor.transpose(xT[:, u, :], x_words[:, u * P : (u + 1) * P], ident[:])
        xT_view = xT[:].rearrange("p u (b i) -> p b i u", b=BATCH)
        xg_words = x_grouped[:].bitcast(F32).rearrange(
            "p (c b i u) -> p c b i u", c=WINDOWS, b=BATCH, u=HALVES
        )
        nc.vector.tensor_copy(out=xg_words[:, 0], in_=xT_view)
        nc.vector.tensor_copy(out=xg_words[:, 1, :, 1:SEQ, :], in_=xT_view[:, :, 0 : SEQ - 1, :])
        nc.vector.tensor_copy(out=xg_words[:, 2, :, 0 : SEQ - 1, :], in_=xT_view[:, :, 1:SEQ, :])
        x_codes = keep.tile([P, WINDOWS, TOK], U32, align_bytes=64)
        x_scales = keep.tile([P, WINDOWS, TOK], U8, align_bytes=64)
        for c in range(WINDOWS):
            nc.vector.quantize_mx(
                out=x_codes[:, c, :].bitcast(FP8X4),
                scales=x_scales[:, c, :],
                in_=x_grouped[:, c * TOK * PACK : (c + 1) * TOK * PACK],
            )

        wl_grouped = keep.tile([P, ITEMS * P * PACK], BF16, align_bytes=64)
        wlg_words = wl_grouped[:].bitcast(F32).rearrange("p (a h u) -> p a h u", a=ITEMS, u=HALVES)
        wl_codes = keep.tile([P, ITEMS * P], U32, align_bytes=64)
        wl_scales = keep.tile([P, ITEMS * P], U8, align_bytes=64)
        for n in range(WL_BANKS):
            wl_words = wl_raw[n][:].bitcast(F32)
            wT = psum_one.tile([P, ITEMS_PER_BANK * HALVES, P], F32, tag="bank")
            for j in range(ITEMS_PER_BANK * HALVES):
                nc.tensor.transpose(wT[:, j, :], wl_words[:, j * P : (j + 1) * P], ident[:])
            nc.scalar.copy(
                out=wlg_words[:, n * ITEMS_PER_BANK : (n + 1) * ITEMS_PER_BANK, :, :],
                in_=wT[:].rearrange("p (a u) h -> p a h u", u=HALVES),
            )
            nc.vector.quantize_mx(
                out=wl_codes[:, n * ITEMS_PER_BANK * P : (n + 1) * ITEMS_PER_BANK * P].bitcast(FP8X4),
                scales=wl_scales[:, n * ITEMS_PER_BANK * P : (n + 1) * ITEMS_PER_BANK * P],
                in_=wl_grouped[:, n * WL_CHUNK : (n + 1) * WL_CHUNK],
            )

        hlT = keep.tile([P, H_TILES, TOK], BF16)

        def layer1_tile(t):
            pre = psum_one.tile([P, TOK], F32, tag="bank")
            for c in range(WINDOWS):
                a = t * WINDOWS + c
                nc.tensor.matmul_mx(
                    out=pre[:],
                    lhsT=wl_codes[:, a * P : (a + 1) * P].bitcast(FP8X4),
                    lhsT_scale=wl_scales[:, a * P : (a + 1) * P],
                    rhs=x_codes[:, c, :].bitcast(FP8X4),
                    rhs_scale=x_scales[:, c, :],
                    start=(c == 0),
                    stop=(c == WINDOWS - 1),
                )
            return pre

        def relu_tile(t, pre):
            nc.scalar.activation(
                out=hlT[:, t, :], in_=pre[:], func=RELU, bias=bias[:, t : t + 1], scale=1.0
            )

        wb_grouped = keep.tile([P, UNITS, UNIT, PACK], BF16, align_bytes=64)
        wb_codes = keep.tile([P, UNITS, UNIT], U32, align_bytes=64)
        wb_scales = keep.tile([P, UNITS, UNIT], U8, align_bytes=64)

        def regroup_unit(q):
            raw = wb_raw[q // UNITS_PER_MAP]
            g0 = (q % UNITS_PER_MAP) * UNIT
            nc.vector.tensor_copy(
                out=wb_grouped[:, q, 0:VECTOR_COLS, :].rearrange("p (c i) t -> p c t i", i=4),
                in_=raw[:, :, g0 : g0 + VECTOR_COLS].rearrange("p t (c i) -> p c t i", i=4),
            )
            nc.scalar.copy(
                out=wb_grouped[:, q, VECTOR_COLS:UNIT, :].rearrange("p (c i) t -> p c t i", i=4),
                in_=raw[:, :, g0 + VECTOR_COLS : g0 + UNIT].rearrange("p t (c i) -> p c t i", i=4),
            )

        def quantise_unit(q):
            nc.vector.quantize_mx(
                out=wb_codes[:, q, :].bitcast(FP8X4),
                scales=wb_scales[:, q, :],
                in_=wb_grouped[:, q, :, :].rearrange("p g t -> p (g t)"),
            )

        hl_grouped = keep.tile([P, TOK, PACK], BF16, align_bytes=64)
        hl_codes = keep.tile([P, TOK], U32, align_bytes=64)
        hl_scales = keep.tile([P, TOK], U8, align_bytes=64)

        def regroup_hl():
            nc.vector.tensor_copy(out=hl_grouped[:], in_=hlT[:].rearrange("p t r -> p r t"))

        def quantise_hl():
            nc.vector.quantize_mx(
                out=hl_codes[:].bitcast(FP8X4),
                scales=hl_scales[:],
                in_=hl_grouped[:].rearrange("p r t -> p (r t)"),
            )

        out_rows = out.rearrange("b i k g -> (b i) (k g)")

        def layer2_unit(q):
            acc = psum_two.tile([P, UNIT], F32)
            nc.tensor.matmul_mx(
                out=acc[:],
                lhsT=hl_codes[:].bitcast(FP8X4),
                lhsT_scale=hl_scales[:],
                rhs=wb_codes[:, q, :].bitcast(FP8X4),
                rhs_scale=wb_scales[:, q, :],
                start=True,
                stop=True,
            )
            result = keep.tile([P, UNIT], F32, name="result%d" % q)
            if q % 2 == 0:
                nc.scalar.copy(out=result[:], in_=acc[:])
            else:
                nc.vector.tensor_copy(out=result[:], in_=acc[:])
            nc.sync.dma_start(out=out_rows[:, q * UNIT : (q + 1) * UNIT], in_=result[:])

        regroup_unit(0)
        for t in range(H_TILES):
            relu_tile(t, layer1_tile(t))
        regroup_unit(1)
        regroup_unit(2)
        quantise_unit(0)
        regroup_hl()
        quantise_unit(1)
        quantise_hl()
        regroup_unit(3)
        quantise_unit(2)
        quantise_unit(3)
        for q in range(UNITS):
            layer2_unit(q)
